import numpy as np
import ml_dtypes


def mxq(x, axis, fmt="e4m3"):
    dtype, down = {"e4m3": (ml_dtypes.float8_e4m3fn, 7), "e5m2": (ml_dtypes.float8_e5m2, 14)}[fmt]
    v = np.moveaxis(np.asarray(x, np.float32).astype(ml_dtypes.bfloat16).astype(np.float64), axis, -1)
    blocks = v.reshape(v.shape[:-1] + (-1, 32))
    amax = np.abs(blocks).max(-1, keepdims=True)
    byte = np.maximum(np.where(amax > 0, np.frexp(amax)[1] - 1 + 127, 0) - down, 1)
    scale = np.exp2(byte - 127.0)
    codes = (blocks / scale).astype(np.float32).astype(dtype).astype(np.float64)
    return np.moveaxis((codes * scale).reshape(v.shape), -1, axis)


WIDE = False


def mx_kscale(k):
    if not WIDE:
        return np.ones(k)
    levels = np.array([10, -10, 5, -5, 0])
    a = np.random.permutation(np.resize(levels, k // 512 * 4)).reshape(k // 512, 4)
    idx = np.arange(k)
    return np.exp2(a[idx // 512, idx % 128 // 32])


BF16 = ml_dtypes.bfloat16


def bf(x):
    return np.asarray(x, np.float32).astype(BF16)


def f64(x):
    return np.asarray(x).astype(np.float64)


N, E, C = 2048, 1024, 512
DENSITY = 0.01
HE_RMS = np.sqrt(np.e / E)


def setup_inputs():
    s, t = mx_kscale(E), mx_kscale(C)
    member = np.random.uniform(size=(N, E)) < DENSITY
    return {"incidence": bf(member * s[None, :]),
            "he": bf(np.random.standard_normal((E, C)) * HE_RMS / s[:, None] * t[None, :]),
            "W2": bf(np.random.standard_normal((C, C)) * 3.0 / np.sqrt(C) / t[:, None]),
            "b2": bf(np.random.standard_normal(C) * 0.2),
            "node_features": bf(np.random.standard_normal((N, C)))}


def reference(incidence, he, W2, b2, node_features):
    prop = mxq(f64(incidence), 1, "e4m3") @ mxq(f64(he), 0, "e4m3")
    return (mxq(prop, 1, "e4m3") @ mxq(f64(W2), 0, "e4m3")) + f64(b2) + f64(node_features)

@@ -1,0 +1,252 @@
+from contextlib import ExitStack
+
+import concourse.mybir as mybir
+from concourse.masks import make_identity
+
+F32 = mybir.dt.float32
+BF16 = mybir.dt.bfloat16
+U32 = mybir.dt.uint32
+U8 = mybir.dt.uint8
+I32 = mybir.dt.int32
+FP8X4 = mybir.dt.float8_e4m3fn_x4
+ADD = mybir.AluOpType.add
+
+P = 128
+N, E, C = 2048, 1024, 512
+NT = N // P
+GT = 2
+NG = NT // GT
+EP = E // 512
+CT = C // P
+
+FLOPS = 2 * N * E * C + 2 * N * C * C
+
+MANUAL = True
+
+
+def tile_heterogeneoustemporalhypergraphnn_pb_kernel(tc, incidence, he, W2, b2, node_features, out):
+    nc = tc.nc
+    with ExitStack() as ctx:
+        if MANUAL:
+            ctx.enter_context(tc.manual_schedule())
+        const = ctx.enter_context(tc.tile_pool(name="const", bufs=1))
+        work = ctx.enter_context(tc.tile_pool(name="work", bufs=3))
+        ps_xt = ctx.enter_context(tc.psum_pool(name="ps_xt", bufs=3))
+        ps_pt = ctx.enter_context(tc.psum_pool(name="ps_pt", bufs=2))
+        ps_po = ctx.enter_context(tc.psum_pool(name="ps_po", bufs=3))
+
+        inc_v = incidence.rearrange("(p r) e -> p r e", r=NT)
+        nf_v = node_features.rearrange("(p r) c -> p r c", r=NT)
+        out_v = out.rearrange("(p r) c -> p r c", r=NT)
+
+        ident = const.tile([P, P], F32)
+        make_identity(nc, ident[:])
+        ones = const.tile([P, P], BF16)
+        nc.vector.memset(ones[:], 1.0)
+        b2pad = const.tile([P, C], BF16)
+        nc.vector.memset(b2pad[:].bitcast(I32), 0)
+
+        he_raw = const.tile([P, EP, 4, C], BF16)
+        he_v = he.rearrange("(g u q e) c -> q g u (e c)", g=EP, u=2, q=P, e=2)
+
+        def load_he(g):
+            nc.sync.dma_start(
+                out=he_raw[:, g].rearrange("p (u e) c -> p u (e c)", u=2), in_=he_v[:, g]
+            )
+
+        inc_raw = []
+        nf_raw = []
+        w2_raw = const.tile([P, CT, C], BF16)
+
+        def load_inc(j):
+            t = const.tile([P, GT, E], BF16, name="inc_raw%d" % j)
+            nc.sync.dma_start(out=t[:], in_=inc_v[:, GT * j : GT * (j + 1), :])
+            inc_raw.append(t)
+
+        def load_nf(k):
+            t = const.tile([P, 4, C], BF16, name="nf_raw%d" % k)
+            nc.sync.dma_start(out=t[:], in_=nf_v[:, 4 * k : 4 * (k + 1), :])
+            nf_raw.append(t)
+
+        load_he(0)
+        load_inc(0)
+        nc.sync.dma_start(out=b2pad[0:1, :], in_=b2.rearrange("(o c) -> o c", o=1))
+        load_he(1)
+        load_nf(0)
+        load_inc(1)
+        nc.sync.dma_start(out=w2_raw[:], in_=W2.rearrange("(t p) n -> p t n", t=CT))
+        load_inc(2)
+        load_inc(3)
+        load_nf(1)
+        load_inc(4)
+        load_inc(5)
+        load_nf(2)
+        load_inc(6)
+        load_inc(7)
+        load_nf(3)
+
+        b2bc = const.tile([P, C], F32)
+
+        def spread_bias():
+            b2ps = ps_po.tile([P, C], F32, tag="po")
+            nc.tensor.matmul(b2ps[:], lhsT=ones[:], rhs=b2pad[:], start=True, stop=True)
+            nc.scalar.copy(out=b2bc[:], in_=b2ps[:])
+
+        he_grp = const.tile([P, EP, C, 4], BF16, align_bytes=64)
+        he_codes = const.tile([P, EP, C], U32, align_bytes=64)
+        he_scales = const.tile([P, EP, C], U8, align_bytes=64)
+        for g in range(EP):
+            nc.vector.tensor_copy(
+                out=he_grp[:, g].rearrange("p (c i) t -> p c t i", i=4),
+                in_=he_raw[:, g].rearrange("p t (c i) -> p c t i", i=4),
+            )
+        for g in range(EP):
+            nc.vector.quantize_mx(
+                out=he_codes[:, g].bitcast(FP8X4),
+                scales=he_scales[:, g],
+                in_=he_grp[:, g].rearrange("p c t -> p (c t)"),
+            )
+
+        w2_grp = const.tile([P, C, 4], BF16, align_bytes=64)
+        w2_codes = const.tile([P, C], U32, align_bytes=64)
+        w2_scales = const.tile([P, C], U8, align_bytes=64)
+
+        def regroup_w2():
+            nc.vector.tensor_copy(
+                out=w2_grp[:].rearrange("p (c i) t -> p c t i", i=4),
+                in_=w2_raw[:].rearrange("p t (c i) -> p c t i", i=4),
+            )
+
+        def quantise_w2():
+            nc.vector.quantize_mx(
+                out=w2_codes[:].bitcast(FP8X4),
+                scales=w2_scales[:],
+                in_=w2_grp[:].rearrange("p c t -> p (c t)"),
+            )
+
+        inc_grp = {}
+        inc_codes = {}
+        inc_scales = {}
+        prop_ps = {}
+        prop_grp = {}
+        prop_codes = {}
+        prop_scales = {}
+        out_ps = {}
+        nfb = {}
+
+        def transpose_group(j):
+            grp = work.tile([P, GT, EP, P, 4], BF16, tag="inc_grp", align_bytes=64)
+            inc_grp[j] = grp
+            banks = []
+            for a in range(GT):
+                xt = ps_xt.tile([P, 2 * EP, P], F32, tag="xt")
+                words = inc_raw[j][:, a, :].bitcast(F32)
+                for w in range(2 * EP):
+                    nc.tensor.transpose(xt[:, w, :], words[:, P * w : P * (w + 1)], ident[:])
+                banks.append(xt)
+            for a in range(GT):
+                nc.scalar.copy(
+                    out=grp[:, a].bitcast(F32),
+                    in_=banks[a][:].rearrange("p (g u) n -> p g n u", u=2),
+                )
+
+        def quantise_inc(j):
+            codes = work.tile([P, GT, EP, P], U32, tag="inc_codes", align_bytes=64)
+            scales = work.tile([P, GT, EP, P], U8, tag="inc_scales", align_bytes=64)
+            inc_codes[j] = codes
+            inc_scales[j] = scales
+            nc.vector.quantize_mx(
+                out=codes[:].rearrange("p a g n -> p (a g n)").bitcast(FP8X4),
+                scales=scales[:].rearrange("p a g n -> p (a g n)"),
+                in_=inc_grp[j][:].rearrange("p a g n t -> p (a g n t)"),
+            )
+
+        def stage1(j):
+            grp = work.tile([P, GT, P, 4], BF16, tag="prop_grp", align_bytes=64)
+            prop_grp[j] = grp
+            banks = []
+            for a in range(GT):
+                pt = ps_pt.tile([P, CT, P], F32, tag="pt")
+                for t in range(CT):
+                    for g in range(EP):
+                        nc.tensor.matmul_mx(
+                            out=pt[:, t, :],
+                            lhsT=he_codes[:, g, P * t : P * (t + 1)].bitcast(FP8X4),
+                            lhsT_scale=he_scales[:, g, P * t : P * (t + 1)],
+                            rhs=inc_codes[j][:, a, g, :].bitcast(FP8X4),
+                            rhs_scale=inc_scales[j][:, a, g, :],
+                            start=(g == 0),
+                            stop=(g == EP - 1),
+                        )
+                banks.append(pt)
+            for a in range(GT):
+                nc.scalar.copy(out=grp[:, a], in_=banks[a][:].rearrange("p t n -> p n t"))
+
+        def quantise_prop(j):
+            codes = work.tile([P, GT, P], U32, tag="prop_codes", align_bytes=64)
+            scales = work.tile([P, GT, P], U8, tag="prop_scales", align_bytes=64)
+            prop_codes[j] = codes
+            prop_scales[j] = scales
+            nc.vector.quantize_mx(
+                out=codes[:].rearrange("p a n -> p (a n)").bitcast(FP8X4),
+                scales=scales[:].rearrange("p a n -> p (a n)"),
+                in_=prop_grp[j][:].rearrange("p a n t -> p (a n t)"),
+            )
+
+        def stage2(j):
+            banks = []
+            for a in range(GT):
+                po = ps_po.tile([P, C], F32, tag="po")
+                nc.tensor.matmul_mx(
+                    out=po[:],
+                    lhsT=prop_codes[j][:, a, :].bitcast(FP8X4),
+                    lhsT_scale=prop_scales[j][:, a, :],
+                    rhs=w2_codes[:].bitcast(FP8X4),
+                    rhs_scale=w2_scales[:],
+                    start=True,
+                    stop=True,
+                )
+                banks.append(po)
+            out_ps[j] = banks
+
+        def pre_add(j):
+            t = const.tile([P, GT, C], F32, name="nfb%d" % j)
+            nfb[j] = t
+            k, h = divmod(j, 2)
+            nc.vector.tensor_tensor(
+                out=t[:],
+                in0=nf_raw[k][:, GT * h : GT * (h + 1), :],
+                in1=b2bc[:].unsqueeze(1).to_broadcast([P, GT, C]),
+                op=ADD,
+            )
+
+        def finish(j):
+            res = const.tile([P, GT, C], F32, name="res%d" % j)
+            for a in range(GT):
+                nc.vector.tensor_tensor(out=res[:, a, :], in0=out_ps[j][a][:], in1=nfb[j][:, a, :], op=ADD)
+                if j == NG - 1:
+                    nc.sync.dma_start(out=out_v[:, GT * j + a, :], in_=res[:, a, :])
+            if j < NG - 1:
+                nc.sync.dma_start(out=out_v[:, GT * j : GT * (j + 1), :], in_=res[:])
+
+        for j in range(NG + 2):
+            if j < NG:
+                transpose_group(j)
+            if j == 0:
+                spread_bias()
+            if 0 <= j - 1 < NG:
+                stage1(j - 1)
+            if 0 <= j - 2 < NG:
+                stage2(j - 2)
+            if j < NG:
+                quantise_inc(j)
+            if j < NG:
+                pre_add(j)
+            if j == 0:
+                regroup_w2()
+            if j == 1:
+                quantise_w2()
+            if 0 <= j - 1 < NG:
+                quantise_prop(j - 1)
+            if 0 <= j - 2 < NG:
+                finish(j - 2)

@@ -213,12 +213,9 @@ def tile_heterogeneoustemporalhypergraphnn_pb_kernel(tc, incidence, he, W2, b2, 
             t = const.tile([P, GT, C], F32, name="nfb%d" % j)
             nfb[j] = t
             k, h = divmod(j, 2)
-            nc.vector.tensor_tensor(
-                out=t[:],
-                in0=nf_raw[k][:, GT * h : GT * (h + 1), :],
-                in1=b2bc[:].unsqueeze(1).to_broadcast([P, GT, C]),
-                op=ADD,
-            )
+            for a in range(GT):
+                eng = nc.gpsimd if a == 1 else nc.vector
+                eng.tensor_tensor(out=t[:, a, :], in0=nf_raw[k][:, GT * h + a, :], in1=b2bc[:], op=ADD)
 
         def finish(j):
             res = const.tile([P, GT, C], F32, name="res%d" % j)

@@ -22,6 +22,7 @@ CT = C // P
 FLOPS = 2 * N * E * C + 2 * N * C * C
 
 MANUAL = True
+ROUTE = "VVVPVVVPVVVPVVVP"
 
 
 def tile_heterogeneoustemporalhypergraphnn_pb_kernel(tc, incidence, he, W2, b2, node_features, out):
@@ -31,9 +32,10 @@ def tile_heterogeneoustemporalhypergraphnn_pb_kernel(tc, incidence, he, W2, b2, 
             ctx.enter_context(tc.manual_schedule())
         const = ctx.enter_context(tc.tile_pool(name="const", bufs=1))
         work = ctx.enter_context(tc.tile_pool(name="work", bufs=3))
-        ps_xt = ctx.enter_context(tc.psum_pool(name="ps_xt", bufs=3))
+        ps_xt = ctx.enter_context(tc.psum_pool(name="ps_xt", bufs=2))
         ps_pt = ctx.enter_context(tc.psum_pool(name="ps_pt", bufs=2))
         ps_po = ctx.enter_context(tc.psum_pool(name="ps_po", bufs=3))
+        ps_pb = ctx.enter_context(tc.psum_pool(name="ps_pb", bufs=1))
 
         inc_v = incidence.rearrange("(p r) e -> p r e", r=NT)
         nf_v = node_features.rearrange("(p r) c -> p r c", r=NT)
@@ -41,6 +43,8 @@ def tile_heterogeneoustemporalhypergraphnn_pb_kernel(tc, incidence, he, W2, b2, 
 
         ident = const.tile([P, P], F32)
         make_identity(nc, ident[:])
+        ident_bf = const.tile([P, P], BF16)
+        make_identity(nc, ident_bf[:])
         ones = const.tile([P, P], BF16)
         nc.vector.memset(ones[:], 1.0)
         b2pad = const.tile([P, C], BF16)
@@ -209,18 +213,33 @@ def tile_heterogeneoustemporalhypergraphnn_pb_kernel(tc, incidence, he, W2, b2, 
                 banks.append(po)
             out_ps[j] = banks
 
-        def pre_add(j):
-            t = const.tile([P, GT, C], F32, name="nfb%d" % j)
-            nfb[j] = t
-            k, h = divmod(j, 2)
+        def nf_tile(t):
+            return nf_raw[t // 4][:, t % 4, :]
+
+        def pre_add_tensor(j):
             for a in range(GT):
-                eng = nc.gpsimd if a == 1 else nc.vector
-                eng.tensor_tensor(out=t[:, a, :], in0=nf_raw[k][:, GT * h + a, :], in1=b2bc[:], op=ADD)
+                t = GT * j + a
+                if ROUTE[t] == "P":
+                    pb = ps_pb.tile([P, C], F32, tag="pb")
+                    nc.tensor.matmul(pb[:], lhsT=ident_bf[:], rhs=nf_tile(t), start=True, stop=False)
+                    nc.tensor.matmul(pb[:], lhsT=ones[:], rhs=b2pad[:], start=False, stop=True)
+                    s = const.tile([P, C], F32, name="nfb%d" % t)
+                    nfb[t] = s
+                    nc.scalar.copy(out=s[:], in_=pb[:])
+
+        def pre_add(j):
+            for a in range(GT):
+                t = GT * j + a
+                if ROUTE[t] != "P":
+                    s = const.tile([P, C], F32, name="nfb%d" % t)
+                    nfb[t] = s
+                    eng = nc.gpsimd if ROUTE[t] == "G" else nc.vector
+                    eng.tensor_tensor(out=s[:], in0=nf_tile(t), in1=b2bc[:], op=ADD)
 
         def finish(j):
             res = const.tile([P, GT, C], F32, name="res%d" % j)
             for a in range(GT):
-                nc.vector.tensor_tensor(out=res[:, a, :], in0=out_ps[j][a][:], in1=nfb[j][:, a, :], op=ADD)
+                nc.vector.tensor_tensor(out=res[:, a, :], in0=out_ps[j][a][:], in1=nfb[GT * j + a][:], op=ADD)
                 if j == NG - 1:
                     nc.sync.dma_start(out=out_v[:, GT * j + a, :], in_=res[:, a, :])
             if j < NG - 1:
@@ -233,6 +252,8 @@ def tile_heterogeneoustemporalhypergraphnn_pb_kernel(tc, incidence, he, W2, b2, 
                 spread_bias()
             if 0 <= j - 1 < NG:
                 stage1(j - 1)
+            if j < NG:
+                pre_add_tensor(j)
             if 0 <= j - 2 < NG:
                 stage2(j - 2)
             if j < NG:

@@ -12,197 +12,161 @@ FP8X4 = mybir.dt.float8_e4m3fn_x4
 ADD = mybir.AluOpType.add
 
 P = 128
+PACK = 4
 N, E, C = 2048, 1024, 512
-NT = N // P
-GT = 2
-NG = NT // GT
-EP = E // 512
-CT = C // P
+TILES = N // P
+GROUP = 2
+GROUPS = TILES // GROUP
+E_PASSES = E // (P * PACK)
+C_TILES = C // P
+NF_LOAD = 4
 
 FLOPS = 2 * N * E * C + 2 * N * C * C
-
-MANUAL = True
-ROUTE = "VVVPVVVPVVVPVVVP"
 
 
 def tile_heterogeneoustemporalhypergraphnn_pb_kernel(tc, incidence, he, W2, b2, node_features, out):
     nc = tc.nc
     with ExitStack() as ctx:
-        if MANUAL:
-            ctx.enter_context(tc.manual_schedule())
-        const = ctx.enter_context(tc.tile_pool(name="const", bufs=1))
-        work = ctx.enter_context(tc.tile_pool(name="work", bufs=3))
-        ps_xt = ctx.enter_context(tc.psum_pool(name="ps_xt", bufs=2))
-        ps_pt = ctx.enter_context(tc.psum_pool(name="ps_pt", bufs=2))
-        ps_po = ctx.enter_context(tc.psum_pool(name="ps_po", bufs=3))
-        ps_pb = ctx.enter_context(tc.psum_pool(name="ps_pb", bufs=1))
+        ctx.enter_context(tc.manual_schedule())
+        keep = ctx.enter_context(tc.tile_pool(name="keep", bufs=1))
+        ring = ctx.enter_context(tc.tile_pool(name="ring", bufs=3))
+        psum_inc = ctx.enter_context(tc.psum_pool(name="psum_inc", bufs=3))
+        psum_prop = ctx.enter_context(tc.psum_pool(name="psum_prop", bufs=2))
+        psum_out = ctx.enter_context(tc.psum_pool(name="psum_out", bufs=3))
 
-        inc_v = incidence.rearrange("(p r) e -> p r e", r=NT)
-        nf_v = node_features.rearrange("(p r) c -> p r c", r=NT)
-        out_v = out.rearrange("(p r) c -> p r c", r=NT)
+        inc_rows = incidence.rearrange("(p r) e -> p r e", r=TILES)
+        nf_rows = node_features.rearrange("(p r) c -> p r c", r=TILES)
+        out_rows = out.rearrange("(p r) c -> p r c", r=TILES)
 
-        ident = const.tile([P, P], F32)
-        make_identity(nc, ident[:])
-        ident_bf = const.tile([P, P], BF16)
-        make_identity(nc, ident_bf[:])
-        ones = const.tile([P, P], BF16)
+        identity = keep.tile([P, P], F32)
+        make_identity(nc, identity[:])
+        ones = keep.tile([P, P], BF16)
         nc.vector.memset(ones[:], 1.0)
-        b2pad = const.tile([P, C], BF16)
-        nc.vector.memset(b2pad[:].bitcast(I32), 0)
+        b2_row0 = keep.tile([P, C], BF16)
+        nc.vector.memset(b2_row0[:].bitcast(I32), 0)
 
-        he_raw = const.tile([P, EP, 4, C], BF16)
-        he_v = he.rearrange("(g u q e) c -> q g u (e c)", g=EP, u=2, q=P, e=2)
-
-        def load_he(g):
-            nc.sync.dma_start(
-                out=he_raw[:, g].rearrange("p (u e) c -> p u (e c)", u=2), in_=he_v[:, g]
-            )
-
+        he_raw = keep.tile([P, E_PASSES, PACK, C], BF16)
+        he_quarters = he.rearrange("(g u p s) c -> p g u (s c)", g=E_PASSES, u=2, p=P, s=2)
+        w2_raw = keep.tile([P, C_TILES, C], BF16)
         inc_raw = []
         nf_raw = []
-        w2_raw = const.tile([P, CT, C], BF16)
 
-        def load_inc(j):
-            t = const.tile([P, GT, E], BF16, name="inc_raw%d" % j)
-            nc.sync.dma_start(out=t[:], in_=inc_v[:, GT * j : GT * (j + 1), :])
-            inc_raw.append(t)
+        def load_he(g):
+            nc.sync.dma_start(out=he_raw[:, g].rearrange("p (u s) c -> p u (s c)", u=2), in_=he_quarters[:, g])
 
-        def load_nf(k):
-            t = const.tile([P, 4, C], BF16, name="nf_raw%d" % k)
-            nc.sync.dma_start(out=t[:], in_=nf_v[:, 4 * k : 4 * (k + 1), :])
-            nf_raw.append(t)
+        def load_incidence(j):
+            raw = keep.tile([P, GROUP, E], BF16, name="inc_raw%d" % j)
+            nc.sync.dma_start(out=raw[:], in_=inc_rows[:, GROUP * j : GROUP * (j + 1), :])
+            inc_raw.append(raw)
+
+        def load_node_features(k):
+            raw = keep.tile([P, NF_LOAD, C], BF16, name="nf_raw%d" % k)
+            nc.sync.dma_start(out=raw[:], in_=nf_rows[:, NF_LOAD * k : NF_LOAD * (k + 1), :])
+            nf_raw.append(raw)
 
         load_he(0)
-        load_inc(0)
-        nc.sync.dma_start(out=b2pad[0:1, :], in_=b2.rearrange("(o c) -> o c", o=1))
         load_he(1)
-        load_nf(0)
-        load_inc(1)
-        nc.sync.dma_start(out=w2_raw[:], in_=W2.rearrange("(t p) n -> p t n", t=CT))
-        load_inc(2)
-        load_inc(3)
-        load_nf(1)
-        load_inc(4)
-        load_inc(5)
-        load_nf(2)
-        load_inc(6)
-        load_inc(7)
-        load_nf(3)
+        load_incidence(0)
+        nc.sync.dma_start(out=b2_row0[0:1, :], in_=b2.rearrange("(o c) -> o c", o=1))
+        load_node_features(0)
+        load_incidence(1)
+        nc.sync.dma_start(out=w2_raw[:], in_=W2.rearrange("(t p) c -> p t c", t=C_TILES))
+        for k in range(1, TILES // NF_LOAD):
+            load_incidence(2 * k)
+            load_incidence(2 * k + 1)
+            load_node_features(k)
 
-        b2bc = const.tile([P, C], F32)
+        he_grouped = keep.tile([P, E_PASSES, C, PACK], BF16, align_bytes=64)
+        he_codes = keep.tile([P, E_PASSES, C], U32, align_bytes=64)
+        he_scales = keep.tile([P, E_PASSES, C], U8, align_bytes=64)
+        w2_grouped = keep.tile([P, C, PACK], BF16, align_bytes=64)
+        w2_codes = keep.tile([P, C], U32, align_bytes=64)
+        w2_scales = keep.tile([P, C], U8, align_bytes=64)
+
+        def regroup(grouped, raw):
+            nc.vector.tensor_copy(
+                out=grouped.rearrange("p (c i) t -> p c t i", i=4), in_=raw.rearrange("p t (c i) -> p c t i", i=4)
+            )
+
+        def quantise(codes, scales, grouped):
+            nc.vector.quantize_mx(out=codes.bitcast(FP8X4), scales=scales, in_=grouped)
+
+        for g in range(E_PASSES):
+            regroup(he_grouped[:, g], he_raw[:, g])
+        for g in range(E_PASSES):
+            quantise(he_codes[:, g], he_scales[:, g], he_grouped[:, g].rearrange("p c t -> p (c t)"))
+
+        b2_all = keep.tile([P, C], F32)
+        inc_grouped, inc_codes, inc_scales = {}, {}, {}
+        prop_grouped, prop_codes, prop_scales = {}, {}, {}
+        out_banks = {}
+        residual = {}
 
         def spread_bias():
-            b2ps = ps_po.tile([P, C], F32, tag="po")
-            nc.tensor.matmul(b2ps[:], lhsT=ones[:], rhs=b2pad[:], start=True, stop=True)
-            nc.scalar.copy(out=b2bc[:], in_=b2ps[:])
+            bank = psum_out.tile([P, C], F32, tag="out_bank")
+            nc.tensor.matmul(bank[:], lhsT=ones[:], rhs=b2_row0[:], start=True, stop=True)
+            nc.scalar.copy(out=b2_all[:], in_=bank[:])
 
-        he_grp = const.tile([P, EP, C, 4], BF16, align_bytes=64)
-        he_codes = const.tile([P, EP, C], U32, align_bytes=64)
-        he_scales = const.tile([P, EP, C], U8, align_bytes=64)
-        for g in range(EP):
-            nc.vector.tensor_copy(
-                out=he_grp[:, g].rearrange("p (c i) t -> p c t i", i=4),
-                in_=he_raw[:, g].rearrange("p t (c i) -> p c t i", i=4),
-            )
-        for g in range(EP):
-            nc.vector.quantize_mx(
-                out=he_codes[:, g].bitcast(FP8X4),
-                scales=he_scales[:, g],
-                in_=he_grp[:, g].rearrange("p c t -> p (c t)"),
-            )
-
-        w2_grp = const.tile([P, C, 4], BF16, align_bytes=64)
-        w2_codes = const.tile([P, C], U32, align_bytes=64)
-        w2_scales = const.tile([P, C], U8, align_bytes=64)
-
-        def regroup_w2():
-            nc.vector.tensor_copy(
-                out=w2_grp[:].rearrange("p (c i) t -> p c t i", i=4),
-                in_=w2_raw[:].rearrange("p t (c i) -> p c t i", i=4),
-            )
-
-        def quantise_w2():
-            nc.vector.quantize_mx(
-                out=w2_codes[:].bitcast(FP8X4),
-                scales=w2_scales[:],
-                in_=w2_grp[:].rearrange("p c t -> p (c t)"),
-            )
-
-        inc_grp = {}
-        inc_codes = {}
-        inc_scales = {}
-        prop_ps = {}
-        prop_grp = {}
-        prop_codes = {}
-        prop_scales = {}
-        out_ps = {}
-        nfb = {}
-
-        def transpose_group(j):
-            grp = work.tile([P, GT, EP, P, 4], BF16, tag="inc_grp", align_bytes=64)
-            inc_grp[j] = grp
+        def transpose_incidence(j):
+            grouped = ring.tile([P, GROUP, E_PASSES, P, PACK], BF16, tag="inc_grouped", align_bytes=64)
+            inc_grouped[j] = grouped
             banks = []
-            for a in range(GT):
-                xt = ps_xt.tile([P, 2 * EP, P], F32, tag="xt")
+            for a in range(GROUP):
+                bank = psum_inc.tile([P, 2 * E_PASSES, P], F32, tag="inc_bank")
                 words = inc_raw[j][:, a, :].bitcast(F32)
-                for w in range(2 * EP):
-                    nc.tensor.transpose(xt[:, w, :], words[:, P * w : P * (w + 1)], ident[:])
-                banks.append(xt)
-            for a in range(GT):
-                nc.scalar.copy(
-                    out=grp[:, a].bitcast(F32),
-                    in_=banks[a][:].rearrange("p (g u) n -> p g n u", u=2),
-                )
+                for w in range(2 * E_PASSES):
+                    nc.tensor.transpose(bank[:, w, :], words[:, P * w : P * (w + 1)], identity[:])
+                banks.append(bank)
+            for a in range(GROUP):
+                nc.scalar.copy(out=grouped[:, a].bitcast(F32), in_=banks[a][:].rearrange("p (g u) n -> p g n u", u=2))
 
-        def quantise_inc(j):
-            codes = work.tile([P, GT, EP, P], U32, tag="inc_codes", align_bytes=64)
-            scales = work.tile([P, GT, EP, P], U8, tag="inc_scales", align_bytes=64)
-            inc_codes[j] = codes
-            inc_scales[j] = scales
-            nc.vector.quantize_mx(
-                out=codes[:].rearrange("p a g n -> p (a g n)").bitcast(FP8X4),
-                scales=scales[:].rearrange("p a g n -> p (a g n)"),
-                in_=inc_grp[j][:].rearrange("p a g n t -> p (a g n t)"),
+        def quantise_incidence(j):
+            codes = ring.tile([P, GROUP, E_PASSES, P], U32, tag="inc_codes", align_bytes=64)
+            scales = ring.tile([P, GROUP, E_PASSES, P], U8, tag="inc_scales", align_bytes=64)
+            inc_codes[j], inc_scales[j] = codes, scales
+            quantise(
+                codes[:].rearrange("p a g n -> p (a g n)"),
+                scales[:].rearrange("p a g n -> p (a g n)"),
+                inc_grouped[j][:].rearrange("p a g n t -> p (a g n t)"),
             )
 
-        def stage1(j):
-            grp = work.tile([P, GT, P, 4], BF16, tag="prop_grp", align_bytes=64)
-            prop_grp[j] = grp
+        def propagate(j):
+            grouped = ring.tile([P, GROUP, P, PACK], BF16, tag="prop_grouped", align_bytes=64)
+            prop_grouped[j] = grouped
             banks = []
-            for a in range(GT):
-                pt = ps_pt.tile([P, CT, P], F32, tag="pt")
-                for t in range(CT):
-                    for g in range(EP):
+            for a in range(GROUP):
+                bank = psum_prop.tile([P, C_TILES, P], F32, tag="prop_bank")
+                for t in range(C_TILES):
+                    for g in range(E_PASSES):
                         nc.tensor.matmul_mx(
-                            out=pt[:, t, :],
+                            out=bank[:, t, :],
                             lhsT=he_codes[:, g, P * t : P * (t + 1)].bitcast(FP8X4),
                             lhsT_scale=he_scales[:, g, P * t : P * (t + 1)],
                             rhs=inc_codes[j][:, a, g, :].bitcast(FP8X4),
                             rhs_scale=inc_scales[j][:, a, g, :],
                             start=(g == 0),
-                            stop=(g == EP - 1),
+                            stop=(g == E_PASSES - 1),
                         )
-                banks.append(pt)
-            for a in range(GT):
-                nc.scalar.copy(out=grp[:, a], in_=banks[a][:].rearrange("p t n -> p n t"))
+                banks.append(bank)
+            for a in range(GROUP):
+                nc.scalar.copy(out=grouped[:, a], in_=banks[a][:].rearrange("p t n -> p n t"))
 
         def quantise_prop(j):
-            codes = work.tile([P, GT, P], U32, tag="prop_codes", align_bytes=64)
-            scales = work.tile([P, GT, P], U8, tag="prop_scales", align_bytes=64)
-            prop_codes[j] = codes
-            prop_scales[j] = scales
-            nc.vector.quantize_mx(
-                out=codes[:].rearrange("p a n -> p (a n)").bitcast(FP8X4),
-                scales=scales[:].rearrange("p a n -> p (a n)"),
-                in_=prop_grp[j][:].rearrange("p a n t -> p (a n t)"),
+            codes = ring.tile([P, GROUP, P], U32, tag="prop_codes", align_bytes=64)
+            scales = ring.tile([P, GROUP, P], U8, tag="prop_scales", align_bytes=64)
+            prop_codes[j], prop_scales[j] = codes, scales
+            quantise(
+                codes[:].rearrange("p a n -> p (a n)"),
+                scales[:].rearrange("p a n -> p (a n)"),
+                prop_grouped[j][:].rearrange("p a n t -> p (a n t)"),
             )
 
-        def stage2(j):
-            banks = []
-            for a in range(GT):
-                po = ps_po.tile([P, C], F32, tag="po")
+        def project(j):
+            out_banks[j] = []
+            for a in range(GROUP):
+                bank = psum_out.tile([P, C], F32, tag="out_bank")
                 nc.tensor.matmul_mx(
-                    out=po[:],
+                    out=bank[:],
                     lhsT=prop_codes[j][:, a, :].bitcast(FP8X4),
                     lhsT_scale=prop_scales[j][:, a, :],
                     rhs=w2_codes[:].bitcast(FP8X4),
@@ -210,61 +174,42 @@ def tile_heterogeneoustemporalhypergraphnn_pb_kernel(tc, incidence, he, W2, b2, 
                     start=True,
                     stop=True,
                 )
-                banks.append(po)
-            out_ps[j] = banks
+                out_banks[j].append(bank)
 
-        def nf_tile(t):
-            return nf_raw[t // 4][:, t % 4, :]
-
-        def pre_add_tensor(j):
-            for a in range(GT):
-                t = GT * j + a
-                if ROUTE[t] == "P":
-                    pb = ps_pb.tile([P, C], F32, tag="pb")
-                    nc.tensor.matmul(pb[:], lhsT=ident_bf[:], rhs=nf_tile(t), start=True, stop=False)
-                    nc.tensor.matmul(pb[:], lhsT=ones[:], rhs=b2pad[:], start=False, stop=True)
-                    s = const.tile([P, C], F32, name="nfb%d" % t)
-                    nfb[t] = s
-                    nc.scalar.copy(out=s[:], in_=pb[:])
-
-        def pre_add(j):
-            for a in range(GT):
-                t = GT * j + a
-                if ROUTE[t] != "P":
-                    s = const.tile([P, C], F32, name="nfb%d" % t)
-                    nfb[t] = s
-                    eng = nc.gpsimd if ROUTE[t] == "G" else nc.vector
-                    eng.tensor_tensor(out=s[:], in0=nf_tile(t), in1=b2bc[:], op=ADD)
+        def add_bias_to_residual(j):
+            residual[j] = []
+            for a, engine in enumerate((nc.vector, nc.gpsimd)):
+                r = GROUP * j + a
+                total = keep.tile([P, C], F32, name="residual%d" % r)
+                engine.tensor_tensor(out=total[:], in0=nf_raw[r // NF_LOAD][:, r % NF_LOAD, :], in1=b2_all[:], op=ADD)
+                residual[j].append(total)
 
         def finish(j):
-            res = const.tile([P, GT, C], F32, name="res%d" % j)
-            for a in range(GT):
-                nc.vector.tensor_tensor(out=res[:, a, :], in0=out_ps[j][a][:], in1=nfb[GT * j + a][:], op=ADD)
-                if j == NG - 1:
-                    nc.sync.dma_start(out=out_v[:, GT * j + a, :], in_=res[:, a, :])
-            if j < NG - 1:
-                nc.sync.dma_start(out=out_v[:, GT * j : GT * (j + 1), :], in_=res[:])
+            result = keep.tile([P, GROUP, C], F32, name="result%d" % j)
+            for a in range(GROUP):
+                nc.vector.tensor_tensor(out=result[:, a, :], in0=out_banks[j][a][:], in1=residual[j][a][:], op=ADD)
+                if j == GROUPS - 1:
+                    nc.sync.dma_start(out=out_rows[:, GROUP * j + a, :], in_=result[:, a, :])
+            if j < GROUPS - 1:
+                nc.sync.dma_start(out=out_rows[:, GROUP * j : GROUP * (j + 1), :], in_=result[:])
 
-        for j in range(NG + 2):
-            if j < NG:
-                transpose_group(j)
+        for j in range(GROUPS + 2):
+            if j < GROUPS:
+                transpose_incidence(j)
             if j == 0:
                 spread_bias()
-            if 0 <= j - 1 < NG:
-                stage1(j - 1)
-            if j < NG:
-                pre_add_tensor(j)
-            if 0 <= j - 2 < NG:
-                stage2(j - 2)
-            if j < NG:
-                quantise_inc(j)
-            if j < NG:
-                pre_add(j)
+            if 1 <= j <= GROUPS:
+                propagate(j - 1)
+            if j >= 2:
+                project(j - 2)
+            if j < GROUPS:
+                quantise_incidence(j)
+                add_bias_to_residual(j)
             if j == 0:
-                regroup_w2()
+                regroup(w2_grouped[:], w2_raw[:])
             if j == 1:
-                quantise_w2()
-            if 0 <= j - 1 < NG:
+                quantise(w2_codes[:], w2_scales[:], w2_grouped[:].rearrange("p c t -> p (c t)"))
+            if 1 <= j <= GROUPS:
                 quantise_prop(j - 1)
-            if 0 <= j - 2 < NG:
+            if j >= 2:
                 finish(j - 2)

@@ -20,6 +20,7 @@ GROUPS = TILES // GROUP
 E_PASSES = E // (P * PACK)
 C_TILES = C // P
 NF_LOAD = 4
+GPSIMD_PIECES = 4
 
 FLOPS = 2 * N * E * C + 2 * N * C * C
 
@@ -178,10 +179,15 @@ def tile_heterogeneoustemporalhypergraphnn_pb_kernel(tc, incidence, he, W2, b2, 
 
         def add_bias_to_residual(j):
             residual[j] = []
-            for a, engine in enumerate((nc.vector, nc.gpsimd)):
+            for a, (engine, pieces) in enumerate(((nc.vector, 1), (nc.gpsimd, GPSIMD_PIECES))):
                 r = GROUP * j + a
                 total = keep.tile([P, C], F32, name="residual%d" % r)
-                engine.tensor_tensor(out=total[:], in0=nf_raw[r // NF_LOAD][:, r % NF_LOAD, :], in1=b2_all[:], op=ADD)
+                width = C // pieces
+                for i in range(pieces):
+                    cols = slice(width * i, width * (i + 1))
+                    engine.tensor_tensor(
+                        out=total[:, cols], in0=nf_raw[r // NF_LOAD][:, r % NF_LOAD, cols], in1=b2_all[:, cols], op=ADD
+                    )
                 residual[j].append(total)
 
         def finish(j):

@@ -20,7 +20,6 @@ GROUPS = TILES // GROUP
 E_PASSES = E // (P * PACK)
 C_TILES = C // P
 NF_LOAD = 4
-GPSIMD_PIECES = 4
 
 FLOPS = 2 * N * E * C + 2 * N * C * C
 
@@ -31,9 +30,10 @@ def tile_heterogeneoustemporalhypergraphnn_pb_kernel(tc, incidence, he, W2, b2, 
         ctx.enter_context(tc.manual_schedule())
         keep = ctx.enter_context(tc.tile_pool(name="keep", bufs=1))
         ring = ctx.enter_context(tc.tile_pool(name="ring", bufs=3))
-        psum_inc = ctx.enter_context(tc.psum_pool(name="psum_inc", bufs=3))
+        psum_inc = ctx.enter_context(tc.psum_pool(name="psum_inc", bufs=2))
         psum_prop = ctx.enter_context(tc.psum_pool(name="psum_prop", bufs=2))
         psum_out = ctx.enter_context(tc.psum_pool(name="psum_out", bufs=3))
+        psum_bias = ctx.enter_context(tc.psum_pool(name="psum_bias", bufs=1))
 
         inc_rows = incidence.rearrange("(p r) e -> p r e", r=TILES)
         nf_rows = node_features.rearrange("(p r) c -> p r c", r=TILES)
@@ -97,6 +97,7 @@ def tile_heterogeneoustemporalhypergraphnn_pb_kernel(tc, incidence, he, W2, b2, 
         for g in range(E_PASSES):
             quantise(he_codes[:, g], he_scales[:, g], he_grouped[:, g].rearrange("p c t -> p (c t)"))
 
+        b2_bank = psum_bias.tile([P, C], F32)
         b2_all = keep.tile([P, C], F32)
         inc_grouped, inc_codes, inc_scales = {}, {}, {}
         prop_grouped, prop_codes, prop_scales = {}, {}, {}
@@ -104,9 +105,8 @@ def tile_heterogeneoustemporalhypergraphnn_pb_kernel(tc, incidence, he, W2, b2, 
         residual = {}
 
         def spread_bias():
-            bank = psum_out.tile([P, C], F32, tag="out_bank")
-            nc.tensor.matmul(bank[:], lhsT=ones[:], rhs=b2_row0[:], start=True, stop=True)
-            nc.scalar.copy(out=b2_all[:], in_=bank[:])
+            nc.tensor.matmul(b2_bank[:], lhsT=ones[:], rhs=b2_row0[:], start=True, stop=True)
+            nc.vector.tensor_copy(out=b2_all[:], in_=b2_bank[:])
 
         def transpose_incidence(j):
             grouped = ring.tile([P, GROUP, E_PASSES, P, PACK], BF16, tag="inc_grouped", align_bytes=64)
@@ -179,15 +179,10 @@ def tile_heterogeneoustemporalhypergraphnn_pb_kernel(tc, incidence, he, W2, b2, 
 
         def add_bias_to_residual(j):
             residual[j] = []
-            for a, (engine, pieces) in enumerate(((nc.vector, 1), (nc.gpsimd, GPSIMD_PIECES))):
+            for a, (engine, bias) in enumerate(((nc.vector, b2_bank), (nc.gpsimd, b2_all))):
                 r = GROUP * j + a
                 total = keep.tile([P, C], F32, name="residual%d" % r)
-                width = C // pieces
-                for i in range(pieces):
-                    cols = slice(width * i, width * (i + 1))
-                    engine.tensor_tensor(
-                        out=total[:, cols], in0=nf_raw[r // NF_LOAD][:, r % NF_LOAD, cols], in1=b2_all[:, cols], op=ADD
-                    )
+                engine.tensor_tensor(out=total[:], in0=nf_raw[r // NF_LOAD][:, r % NF_LOAD, :], in1=bias[:], op=ADD)
                 residual[j].append(total)
 
         def finish(j):

@@ -27,13 +27,11 @@ FLOPS = 2 * N * E * C + 2 * N * C * C
 def tile_heterogeneoustemporalhypergraphnn_pb_kernel(tc, incidence, he, W2, b2, node_features, out):
     nc = tc.nc
     with ExitStack() as ctx:
-        ctx.enter_context(tc.manual_schedule())
         keep = ctx.enter_context(tc.tile_pool(name="keep", bufs=1))
         ring = ctx.enter_context(tc.tile_pool(name="ring", bufs=3))
-        psum_inc = ctx.enter_context(tc.psum_pool(name="psum_inc", bufs=2))
+        psum_inc = ctx.enter_context(tc.psum_pool(name="psum_inc", bufs=3))
         psum_prop = ctx.enter_context(tc.psum_pool(name="psum_prop", bufs=2))
         psum_out = ctx.enter_context(tc.psum_pool(name="psum_out", bufs=3))
-        psum_bias = ctx.enter_context(tc.psum_pool(name="psum_bias", bufs=1))
 
         inc_rows = incidence.rearrange("(p r) e -> p r e", r=TILES)
         nf_rows = node_features.rearrange("(p r) c -> p r c", r=TILES)
@@ -97,7 +95,6 @@ def tile_heterogeneoustemporalhypergraphnn_pb_kernel(tc, incidence, he, W2, b2, 
         for g in range(E_PASSES):
             quantise(he_codes[:, g], he_scales[:, g], he_grouped[:, g].rearrange("p c t -> p (c t)"))
 
-        b2_bank = psum_bias.tile([P, C], F32)
         b2_all = keep.tile([P, C], F32)
         inc_grouped, inc_codes, inc_scales = {}, {}, {}
         prop_grouped, prop_codes, prop_scales = {}, {}, {}
@@ -105,8 +102,9 @@ def tile_heterogeneoustemporalhypergraphnn_pb_kernel(tc, incidence, he, W2, b2, 
         residual = {}
 
         def spread_bias():
-            nc.tensor.matmul(b2_bank[:], lhsT=ones[:], rhs=b2_row0[:], start=True, stop=True)
-            nc.vector.tensor_copy(out=b2_all[:], in_=b2_bank[:])
+            bank = psum_out.tile([P, C], F32, tag="out_bank")
+            nc.tensor.matmul(bank[:], lhsT=ones[:], rhs=b2_row0[:], start=True, stop=True)
+            nc.scalar.copy(out=b2_all[:], in_=bank[:])
 
         def transpose_incidence(j):
             grouped = ring.tile([P, GROUP, E_PASSES, P, PACK], BF16, tag="inc_grouped", align_bytes=64)
@@ -179,10 +177,10 @@ def tile_heterogeneoustemporalhypergraphnn_pb_kernel(tc, incidence, he, W2, b2, 
 
         def add_bias_to_residual(j):
             residual[j] = []
-            for a, (engine, bias) in enumerate(((nc.vector, b2_bank), (nc.gpsimd, b2_all))):
+            for a, engine in enumerate((nc.vector, nc.gpsimd)):
                 r = GROUP * j + a
                 total = keep.tile([P, C], F32, name="residual%d" % r)
-                engine.tensor_tensor(out=total[:], in0=nf_raw[r // NF_LOAD][:, r % NF_LOAD, :], in1=bias[:], op=ADD)
+                engine.tensor_tensor(out=total[:], in0=nf_raw[r // NF_LOAD][:, r % NF_LOAD, :], in1=b2_all[:], op=ADD)
                 residual[j].append(total)
 
         def finish(j):

from contextlib import ExitStack

import concourse.mybir as mybir
from concourse.masks import make_identity

F32 = mybir.dt.float32
BF16 = mybir.dt.bfloat16
U32 = mybir.dt.uint32
U8 = mybir.dt.uint8
I32 = mybir.dt.int32
FP8X4 = mybir.dt.float8_e4m3fn_x4
ADD = mybir.AluOpType.add

P = 128
PACK = 4
N, E, C = 2048, 1024, 512
TILES = N // P
GROUP = 2
GROUPS = TILES // GROUP
E_PASSES = E // (P * PACK)
C_TILES = C // P
NF_LOAD = 4

FLOPS = 2 * N * E * C + 2 * N * C * C


def tile_heterogeneoustemporalhypergraphnn_pb_kernel(tc, incidence, he, W2, b2, node_features, out):
    nc = tc.nc
    with ExitStack() as ctx:
        keep = ctx.enter_context(tc.tile_pool(name="keep", bufs=1))
        ring = ctx.enter_context(tc.tile_pool(name="ring", bufs=3))
        psum_inc = ctx.enter_context(tc.psum_pool(name="psum_inc", bufs=3))
        psum_prop = ctx.enter_context(tc.psum_pool(name="psum_prop", bufs=2))
        psum_out = ctx.enter_context(tc.psum_pool(name="psum_out", bufs=3))

        inc_rows = incidence.rearrange("(p r) e -> p r e", r=TILES)
        nf_rows = node_features.rearrange("(p r) c -> p r c", r=TILES)
        out_rows = out.rearrange("(p r) c -> p r c", r=TILES)

        identity = keep.tile([P, P], F32)
        make_identity(nc, identity[:])
        ones = keep.tile([P, P], BF16)
        nc.vector.memset(ones[:], 1.0)
        b2_row0 = keep.tile([P, C], BF16)
        nc.vector.memset(b2_row0[:].bitcast(I32), 0)

        he_raw = keep.tile([P, E_PASSES, PACK, C], BF16)
        he_quarters = he.rearrange("(g u p s) c -> p g u (s c)", g=E_PASSES, u=2, p=P, s=2)
        w2_raw = keep.tile([P, C_TILES, C], BF16)
        inc_raw = []
        nf_raw = []

        def load_he(g):
            nc.sync.dma_start(out=he_raw[:, g].rearrange("p (u s) c -> p u (s c)", u=2), in_=he_quarters[:, g])

        def load_incidence(j):
            raw = keep.tile([P, GROUP, E], BF16, name="inc_raw%d" % j)
            nc.sync.dma_start(out=raw[:], in_=inc_rows[:, GROUP * j : GROUP * (j + 1), :])
            inc_raw.append(raw)

        def load_node_features(k):
            raw = keep.tile([P, NF_LOAD, C], BF16, name="nf_raw%d" % k)
            nc.sync.dma_start(out=raw[:], in_=nf_rows[:, NF_LOAD * k : NF_LOAD * (k + 1), :])
            nf_raw.append(raw)

        load_he(0)
        load_he(1)
        load_incidence(0)
        nc.sync.dma_start(out=b2_row0[0:1, :], in_=b2.rearrange("(o c) -> o c", o=1))
        load_node_features(0)
        load_incidence(1)
        nc.sync.dma_start(out=w2_raw[:], in_=W2.rearrange("(t p) c -> p t c", t=C_TILES))
        for k in range(1, TILES // NF_LOAD):
            load_incidence(2 * k)
            load_incidence(2 * k + 1)
            load_node_features(k)

        he_grouped = keep.tile([P, E_PASSES, C, PACK], BF16, align_bytes=64)
        he_codes = keep.tile([P, E_PASSES, C], U32, align_bytes=64)
        he_scales = keep.tile([P, E_PASSES, C], U8, align_bytes=64)
        w2_grouped = keep.tile([P, C, PACK], BF16, align_bytes=64)
        w2_codes = keep.tile([P, C], U32, align_bytes=64)
        w2_scales = keep.tile([P, C], U8, align_bytes=64)

        def regroup(grouped, raw):
            nc.vector.tensor_copy(
                out=grouped.rearrange("p (c i) t -> p c t i", i=4), in_=raw.rearrange("p t (c i) -> p c t i", i=4)
            )

        def quantise(codes, scales, grouped):
            nc.vector.quantize_mx(out=codes.bitcast(FP8X4), scales=scales, in_=grouped)

        for g in range(E_PASSES):
            regroup(he_grouped[:, g], he_raw[:, g])
        for g in range(E_PASSES):
            quantise(he_codes[:, g], he_scales[:, g], he_grouped[:, g].rearrange("p c t -> p (c t)"))

        b2_all = keep.tile([P, C], F32)
        inc_grouped, inc_codes, inc_scales = {}, {}, {}
        prop_grouped, prop_codes, prop_scales = {}, {}, {}
        out_banks = {}
        residual = {}

        def spread_bias():
            bank = psum_out.tile([P, C], F32, tag="out_bank")
            nc.tensor.matmul(bank[:], lhsT=ones[:], rhs=b2_row0[:], start=True, stop=True)
            nc.scalar.copy(out=b2_all[:], in_=bank[:])

        def transpose_incidence(j):
            grouped = ring.tile([P, GROUP, E_PASSES, P, PACK], BF16, tag="inc_grouped", align_bytes=64)
            inc_grouped[j] = grouped
            banks = []
            for a in range(GROUP):
                bank = psum_inc.tile([P, 2 * E_PASSES, P], F32, tag="inc_bank")
                words = inc_raw[j][:, a, :].bitcast(F32)
                for w in range(2 * E_PASSES):
                    nc.tensor.transpose(bank[:, w, :], words[:, P * w : P * (w + 1)], identity[:])
                banks.append(bank)
            for a in range(GROUP):
                nc.scalar.copy(out=grouped[:, a].bitcast(F32), in_=banks[a][:].rearrange("p (g u) n -> p g n u", u=2))

        def quantise_incidence(j):
            codes = ring.tile([P, GROUP, E_PASSES, P], U32, tag="inc_codes", align_bytes=64)
            scales = ring.tile([P, GROUP, E_PASSES, P], U8, tag="inc_scales", align_bytes=64)
            inc_codes[j], inc_scales[j] = codes, scales
            quantise(
                codes[:].rearrange("p a g n -> p (a g n)"),
                scales[:].rearrange("p a g n -> p (a g n)"),
                inc_grouped[j][:].rearrange("p a g n t -> p (a g n t)"),
            )

        def propagate(j):
            grouped = ring.tile([P, GROUP, P, PACK], BF16, tag="prop_grouped", align_bytes=64)
            prop_grouped[j] = grouped
            banks = []
            for a in range(GROUP):
                bank = psum_prop.tile([P, C_TILES, P], F32, tag="prop_bank")
                for t in range(C_TILES):
                    for g in range(E_PASSES):
                        nc.tensor.matmul_mx(
                            out=bank[:, t, :],
                            lhsT=he_codes[:, g, P * t : P * (t + 1)].bitcast(FP8X4),
                            lhsT_scale=he_scales[:, g, P * t : P * (t + 1)],
                            rhs=inc_codes[j][:, a, g, :].bitcast(FP8X4),
                            rhs_scale=inc_scales[j][:, a, g, :],
                            start=(g == 0),
                            stop=(g == E_PASSES - 1),
                        )
                banks.append(bank)
            for a in range(GROUP):
                nc.scalar.copy(out=grouped[:, a], in_=banks[a][:].rearrange("p t n -> p n t"))

        def quantise_prop(j):
            codes = ring.tile([P, GROUP, P], U32, tag="prop_codes", align_bytes=64)
            scales = ring.tile([P, GROUP, P], U8, tag="prop_scales", align_bytes=64)
            prop_codes[j], prop_scales[j] = codes, scales
            quantise(
                codes[:].rearrange("p a n -> p (a n)"),
                scales[:].rearrange("p a n -> p (a n)"),
                prop_grouped[j][:].rearrange("p a n t -> p (a n t)"),
            )

        def project(j):
            out_banks[j] = []
            for a in range(GROUP):
                bank = psum_out.tile([P, C], F32, tag="out_bank")
                nc.tensor.matmul_mx(
                    out=bank[:],
                    lhsT=prop_codes[j][:, a, :].bitcast(FP8X4),
                    lhsT_scale=prop_scales[j][:, a, :],
                    rhs=w2_codes[:].bitcast(FP8X4),
                    rhs_scale=w2_scales[:],
                    start=True,
                    stop=True,
                )
                out_banks[j].append(bank)

        def add_bias_to_residual(j):
            residual[j] = []
            for a, engine in enumerate((nc.vector, nc.gpsimd)):
                r = GROUP * j + a
                total = keep.tile([P, C], F32, name="residual%d" % r)
                engine.tensor_tensor(out=total[:], in0=nf_raw[r // NF_LOAD][:, r % NF_LOAD, :], in1=b2_all[:], op=ADD)
                residual[j].append(total)

        def finish(j):
            result = keep.tile([P, GROUP, C], F32, name="result%d" % j)
            for a in range(GROUP):
                nc.vector.tensor_tensor(out=result[:, a, :], in0=out_banks[j][a][:], in1=residual[j][a][:], op=ADD)
                if j == GROUPS - 1:
                    nc.sync.dma_start(out=out_rows[:, GROUP * j + a, :], in_=result[:, a, :])
            if j < GROUPS - 1:
                nc.sync.dma_start(out=out_rows[:, GROUP * j : GROUP * (j + 1), :], in_=result[:])

        for j in range(GROUPS + 2):
            if j < GROUPS:
                transpose_incidence(j)
            if j == 0:
                spread_bias()
            if 1 <= j <= GROUPS:
                propagate(j - 1)
            if j >= 2:
                project(j - 2)
            if j < GROUPS:
                quantise_incidence(j)
                add_bias_to_residual(j)
            if j == 0:
                regroup(w2_grouped[:], w2_raw[:])
            if j == 1:
                quantise(w2_codes[:], w2_scales[:], w2_grouped[:].rearrange("p c t -> p (c t)"))
            if 1 <= j <= GROUPS:
                quantise_prop(j - 1)
            if j >= 2:
                finish(j - 2)
